import numpy as np
import ml_dtypes


def mxq(x, axis, fmt="e4m3"):
    dtype, down = {"e4m3": (ml_dtypes.float8_e4m3fn, 7), "e5m2": (ml_dtypes.float8_e5m2, 14)}[fmt]
    v = np.moveaxis(np.asarray(x, np.float32).astype(ml_dtypes.bfloat16).astype(np.float64), axis, -1)
    blocks = v.reshape(v.shape[:-1] + (-1, 32))
    amax = np.abs(blocks).max(-1, keepdims=True)
    byte = np.maximum(np.where(amax > 0, np.frexp(amax)[1] - 1 + 127, 0) - down, 1)
    scale = np.exp2(byte - 127.0)
    codes = (blocks / scale).astype(np.float32).astype(dtype).astype(np.float64)
    return np.moveaxis((codes * scale).reshape(v.shape), -1, axis)


WIDE = False


def mx_kscale(k):
    if not WIDE:
        return np.ones(k)
    levels = np.array([10, -10, 5, -5, 0])
    a = np.random.permutation(np.resize(levels, k // 512 * 4)).reshape(k // 512, 4)
    idx = np.arange(k)
    return np.exp2(a[idx // 512, idx % 128 // 32])


BF16 = ml_dtypes.bfloat16


def bf(x):
    return np.asarray(x, np.float32).astype(BF16)


def f64(x):
    return np.asarray(x).astype(np.float64)


B, W, U, H, D, K, MAX_BACK, MAX_FWD = 2, 4, 128, 4, 512, 256, 127, 0
CH = H * D
F = MAX_BACK + MAX_FWD + 1


def setup_inputs():
    s, t = mx_kscale(CH), mx_kscale(D)
    a = 1.5 * D ** -0.25
    return {"queries": bf(np.random.standard_normal((B, W, U, H, D)) * a * t),
            "keys": bf(np.random.standard_normal((B, W, K, H, D)) * a / t),
            "sin_emb": bf(np.random.standard_normal((F, CH)) * np.sqrt(0.5) * s),
            "pos_w": bf(np.random.standard_normal((CH, CH)) * 2.0 * D ** -0.25 / np.sqrt(CH) / s[None, :] / np.tile(t, H)[:, None])}


def relative_shift(x):
    pad = K + 1 - F
    x = np.pad(x, ((0, 0), (0, 0), (0, 0), (0, 0), (0, pad)))
    x = x.reshape(B, H, W, U * (K + 1))[:, :, :, : U * K]
    return x.reshape(B, H, W, U, K)


def reference(queries, keys, sin_emb, pos_w):
    proj = (mxq(f64(sin_emb), 1, "e4m3") @ mxq(f64(pos_w), 1, "e4m3").T).reshape(F, H, D)
    qq = mxq(f64(queries), 4, "e4m3").transpose(0, 3, 1, 2, 4)
    kq = mxq(f64(keys), 4, "e4m3").transpose(0, 3, 1, 4, 2)
    pq = mxq(proj, 2, "e4m3").transpose(1, 2, 0)[None, :, None]
    term_ac = qq @ kq
    term_bd = qq @ pq
    return term_ac + relative_shift(term_bd)

@@ -1,0 +1,213 @@
+from contextlib import ExitStack
+
+import concourse.mybir as mybir
+from concourse.masks import make_identity
+
+F32 = mybir.dt.float32
+BF16 = mybir.dt.bfloat16
+U32 = mybir.dt.uint32
+U8 = mybir.dt.uint8
+FP8X4 = mybir.dt.float8_e4m3fn_x4
+
+P = 128
+B, W, U, H, D, KC, F = 2, 4, 128, 4, 512, 256, 128
+CH = H * D
+PITCH = 160
+WIN = 159
+QUAD = 32
+GROUPS = U // QUAD
+BLOCK = U * PITCH
+SCRATCH = B * H * W * U * KC - B * W * H * BLOCK
+
+FLOPS = 2 * F * CH * CH + B * W * H * 2 * U * D * (KC + F)
+
+
+def tile_gemma3naudiorelativepositionembedding_pa_kernel(tc, queries, keys, sin_emb, pos_w, out):
+    nc = tc.nc
+    with ExitStack() as ctx:
+        const = ctx.enter_context(tc.tile_pool(name="const", bufs=1))
+        raw = ctx.enter_context(tc.tile_pool(name="raw", bufs=8))
+        qin = ctx.enter_context(tc.tile_pool(name="qin", bufs=3))
+        grp = ctx.enter_context(tc.tile_pool(name="grp", bufs=2))
+        cod = ctx.enter_context(tc.tile_pool(name="cod", bufs=2))
+        kcd = ctx.enter_context(tc.tile_pool(name="kcd", bufs=3))
+        outp = ctx.enter_context(tc.tile_pool(name="outp", bufs=3))
+        psum_t = ctx.enter_context(tc.psum_pool(name="psumt", bufs=4))
+        psum_a = ctx.enter_context(tc.psum_pool(name="psuma", bufs=4))
+
+        ident = const.tile([P, P], F32)
+        make_identity(nc, ident[:])
+
+        perm = const.tile([P, P], F32)
+        nc.vector.tensor_copy(
+            out=perm[:].rearrange("p (r a) -> p a r", a=GROUPS), in_=ident[:].rearrange("p (a r) -> p a r", a=GROUPS)
+        )
+        shifted = const.tile([P, B * W * H, KC], F32)
+        for j in range(4):
+            nc.vector.memset(shifted[:, 8 * j : 8 * j + 8, :], 0.0)
+        outflat = out.rearrange("b h w u c -> (b h w u c)")
+        stages = []
+        for n in range(4):
+            stage = const.tile([P, H, PITCH], F32, name="stage%d" % n)
+            nc.vector.memset(stage[:, :, F:PITCH], 0.0)
+            stages.append(stage)
+
+        qcodes = const.tile([P, B * W, H * U], U32, align_bytes=64)
+        qscales = const.tile([P, B * W, H * U], U8, align_bytes=64)
+        scodes = const.tile([P, 4 * F], U32, align_bytes=64)
+        sscales = const.tile([P, 4 * F], U8, align_bytes=64)
+        pcodes = const.tile([P, H * F], U32, align_bytes=64)
+        pscales = const.tile([P, H * F], U8, align_bytes=64)
+
+        counter = [0]
+
+        def transpose_bank(words, first, eye):
+            bank = psum_t.tile([P, 2, 2, P], F32, tag="xt")
+            for x in range(2):
+                for u in range(2):
+                    j = first + 2 * x + u
+                    nc.tensor.transpose(bank[:, x, u, :], words[:, j * P : (j + 1) * P], eye[:])
+            return bank
+
+        def evacuate(dst, bank, vector_every):
+            src = bank[:].rearrange("p x u r -> p x r u")
+            counter[0] += 1
+            if vector_every and counter[0] % vector_every == 0:
+                nc.vector.tensor_copy(out=dst, in_=src)
+            else:
+                nc.scalar.copy(out=dst, in_=src)
+
+        sraw = const.tile([P, CH], BF16)
+        nc.sync.dma_start(out=sraw[:], in_=sin_emb)
+        gs = grp.tile([P, 4, P, 4], BF16, tag="gq", align_bytes=64)
+        for i in range(2):
+            bank = transpose_bank(sraw[:].bitcast(F32), 4 * i, ident)
+            evacuate(gs[:].bitcast(F32)[:, 2 * i : 2 * i + 2, :, :], bank, 2)
+        nc.vector.quantize_mx(
+            out=scodes[:].bitcast(FP8X4), scales=sscales[:], in_=gs[:].rearrange("p c r t -> p (c r t)")
+        )
+
+        pbank = None
+        for g in range(8):
+            h = g // 2
+            wraw = raw.tile([P, 2, CH], BF16, tag="raw8")
+            nc.sync.dma_start(out=wraw[:], in_=pos_w[256 * g : 256 * (g + 1), :].rearrange("(p e) c -> p e c", e=2))
+            gw = grp.tile([P, 2, 4, P, 4], BF16, tag="gw", align_bytes=64)
+            wcodes = cod.tile([P, 2, 4 * P], U32, align_bytes=64)
+            wscales = cod.tile([P, 2, 4 * P], U8, align_bytes=64)
+            if g % 2 == 0:
+                pbank = psum_a.tile([P, 4, F], F32, tag="acc")
+            for e in range(2):
+                for i in range(2):
+                    bank = transpose_bank(wraw[:, e, :].bitcast(F32), 4 * i, ident)
+                    evacuate(gw[:, e].bitcast(F32)[:, 2 * i : 2 * i + 2, :, :], bank, 4)
+                nc.vector.quantize_mx(
+                    out=wcodes[:, e, :].bitcast(FP8X4),
+                    scales=wscales[:, e, :],
+                    in_=gw[:, e].rearrange("p c r t -> p (c r t)"),
+                )
+            for e in range(2):
+                t = 2 * (g % 2) + e
+                for c in range(4):
+                    cols = slice(c * P, (c + 1) * P)
+                    nc.tensor.matmul_mx(
+                        out=pbank[:, t, :],
+                        lhsT=wcodes[:, e, cols].bitcast(FP8X4),
+                        lhsT_scale=wscales[:, e, cols],
+                        rhs=scodes[:, cols].bitcast(FP8X4),
+                        rhs_scale=sscales[:, cols],
+                        start=(c == 0),
+                        stop=(c == 3),
+                    )
+            if g % 2 == 0:
+                continue
+            hcols = slice(h * P, (h + 1) * P)
+            pg = grp.tile([P, F, 4], BF16, tag="pg", align_bytes=64)
+            nc.vector.tensor_copy(out=pg[:], in_=pbank[:].rearrange("p t f -> p f t"))
+            nc.vector.quantize_mx(
+                out=pcodes[:, hcols].bitcast(FP8X4), scales=pscales[:, hcols], in_=pg[:].rearrange("p f t -> p (f t)")
+            )
+
+        for bw in range(B * W):
+            qraw = qin.tile([P, CH], BF16)
+            nc.sync.dma_start(out=qraw[:], in_=queries[bw // W, bw % W].rearrange("u h d -> u (h d)"))
+            gq = grp.tile([P, H, P, 4], BF16, tag="gq", align_bytes=64)
+            for i in range(2):
+                bank = transpose_bank(qraw[:].bitcast(F32), 4 * i, perm)
+                evacuate(gq[:].bitcast(F32)[:, 2 * i : 2 * i + 2, :, :], bank, 2)
+            nc.vector.quantize_mx(
+                out=qcodes[:, bw, :].bitcast(FP8X4),
+                scales=qscales[:, bw, :],
+                in_=gq[:].rearrange("p h r t -> p (h r t)"),
+            )
+
+            bdbank = psum_a.tile([P, H, F], F32, tag="acc")
+            for h in range(H):
+                hcols = slice(h * P, (h + 1) * P)
+                nc.tensor.matmul_mx(
+                    out=bdbank[:, h, :],
+                    lhsT=qcodes[:, bw, hcols].bitcast(FP8X4),
+                    lhsT_scale=qscales[:, bw, hcols],
+                    rhs=pcodes[:, hcols].bitcast(FP8X4),
+                    rhs_scale=pscales[:, hcols],
+                    start=True,
+                    stop=True,
+                )
+            stage = stages[bw % 4]
+            nc.scalar.copy(out=stage[:, :, 0:F], in_=bdbank[:])
+            first = SCRATCH + bw * H * BLOCK
+            nc.scalar.dma_start(
+                out=outflat[first : first + H * BLOCK].rearrange("(h u x) -> u h x", h=H, x=PITCH), in_=stage[:]
+            )
+            if bw % 2 == 0:
+                continue
+            first = SCRATCH + (bw - 1) * H * BLOCK
+            rows = (
+                outflat[first : first + 2 * H * BLOCK]
+                .rearrange("(k y) -> k y", k=2 * H)[:, 0 : QUAD * (GROUPS * PITCH - 1)]
+                .rearrange("k (r x) -> r k x", x=GROUPS * PITCH - 1)
+            )
+            for a in range(GROUPS):
+                nc.sync.dma_start(
+                    out=shifted[a:P:GROUPS, (bw - 1) * H : (bw + 1) * H, a * QUAD : a * QUAD + WIN],
+                    in_=rows[:, :, a * PITCH : a * PITCH + WIN],
+                )
+
+        for bw in range(B * W):
+            b, w = bw // W, bw % W
+            kraw = raw.tile([P, 2, CH], BF16, tag="raw8")
+            nc.sync.dma_start(out=kraw[:], in_=keys[b, w].rearrange("(e p) h d -> p e (h d)", e=2))
+            total = outp.tile([P, H, KC], F32)
+            for i in range(2):
+                gk = grp.tile([P, 2, KC, 4], BF16, tag="gk", bufs=3, align_bytes=64)
+                for e in range(2):
+                    bank = transpose_bank(kraw[:, e, :].bitcast(F32), 4 * i, ident)
+                    evacuate(gk[:].bitcast(F32)[:, :, e * P : (e + 1) * P, :], bank, 0)
+                kcodes = kcd.tile([P, 2 * KC], U32, align_bytes=64)
+                kscales = kcd.tile([P, 2 * KC], U8, align_bytes=64)
+                nc.vector.quantize_mx(
+                    out=kcodes[:].bitcast(FP8X4), scales=kscales[:], in_=gk[:].rearrange("p x c t -> p (x c t)")
+                )
+                acbank = psum_a.tile([P, 2, KC], F32, tag="acc")
+                for x in range(2):
+                    hcols = slice((2 * i + x) * P, (2 * i + x + 1) * P)
+                    kcols = slice(x * KC, (x + 1) * KC)
+                    nc.tensor.matmul_mx(
+                        out=acbank[:, x, :],
+                        lhsT=qcodes[:, bw, hcols].bitcast(FP8X4),
+                        lhsT_scale=qscales[:, bw, hcols],
+                        rhs=kcodes[:, kcols].bitcast(FP8X4),
+                        rhs_scale=kscales[:, kcols],
+                        start=True,
+                        stop=True,
+                    )
+                nc.vector.tensor_tensor(
+                    out=total[:, 2 * i : 2 * i + 2, :],
+                    in0=acbank[:],
+                    in1=shifted[:, bw * H + 2 * i : bw * H + 2 * i + 2, :],
+                    op=mybir.AluOpType.add,
+                )
+            for a in range(GROUPS):
+                nc.sync.dma_start(
+                    out=out[b, :, w, a * QUAD : (a + 1) * QUAD, :].rearrange("h r c -> r h c"), in_=total[a:P:GROUPS, :, :]
+                )

@@ -13,11 +13,16 @@ P = 128
 B, W, U, H, D, KC, F = 2, 4, 128, 4, 512, 256, 128
 CH = H * D
 PITCH = 160
-WIN = 159
+WIN = PITCH - 1
 QUAD = 32
 GROUPS = U // QUAD
-BLOCK = U * PITCH
-SCRATCH = B * H * W * U * KC - B * W * H * BLOCK
+PAIR_ROW = 2 * H * PITCH
+PAIR = U * PAIR_ROW
+SCRATCH = B * H * W * U * KC - 4 * PAIR - 4096
+
+N_W, N_Q, N_K = 8, 4, 8
+N_TILES = N_W + N_Q + N_K
+DEPTH = 8
 
 FLOPS = 2 * F * CH * CH + B * W * H * 2 * U * D * (KC + F)
 
@@ -26,188 +31,202 @@ def tile_gemma3naudiorelativepositionembedding_pa_kernel(tc, queries, keys, sin_
     nc = tc.nc
     with ExitStack() as ctx:
         const = ctx.enter_context(tc.tile_pool(name="const", bufs=1))
-        raw = ctx.enter_context(tc.tile_pool(name="raw", bufs=8))
-        qin = ctx.enter_context(tc.tile_pool(name="qin", bufs=3))
-        grp = ctx.enter_context(tc.tile_pool(name="grp", bufs=2))
-        cod = ctx.enter_context(tc.tile_pool(name="cod", bufs=2))
-        kcd = ctx.enter_context(tc.tile_pool(name="kcd", bufs=3))
+        rawp = ctx.enter_context(tc.tile_pool(name="rawp", bufs=DEPTH))
+        grp = ctx.enter_context(tc.tile_pool(name="grp", bufs=3))
+        cod = ctx.enter_context(tc.tile_pool(name="cod", bufs=3))
         outp = ctx.enter_context(tc.tile_pool(name="outp", bufs=3))
         psum_t = ctx.enter_context(tc.psum_pool(name="psumt", bufs=4))
         psum_a = ctx.enter_context(tc.psum_pool(name="psuma", bufs=4))
+        ctx.enter_context(tc.manual_schedule())
+
+        outflat = out.rearrange("b h w u c -> (b h w u c)")
+        raw, grouped, codes, scales, banks = {}, {}, {}, {}, {}
+
+        def load(t):
+            raw[t] = rawp.tile([P, 2, CH], BF16, name="raw", tag="raw")
+            if t < N_W:
+                src = pos_w[256 * t : 256 * (t + 1), :].rearrange("(p e) c -> p e c", e=2)
+            elif t < N_W + N_Q:
+                j = t - N_W
+                src = queries[j // 2, 2 * (j % 2) : 2 * (j % 2) + 2].rearrange("s u h d -> u s (h d)")
+            else:
+                bw = t - N_W - N_Q
+                src = keys[bw // W, bw % W].rearrange("(p e) h d -> p e (h d)", e=2)
+            nc.sync.dma_start(out=raw[t][:], in_=src)
+
+        sraw = const.tile([P, CH], BF16)
+        nc.sync.dma_start(out=sraw[:], in_=sin_emb)
+        for t in range(DEPTH):
+            load(t)
 
         ident = const.tile([P, P], F32)
         make_identity(nc, ident[:])
-
         perm = const.tile([P, P], F32)
         nc.vector.tensor_copy(
             out=perm[:].rearrange("p (r a) -> p a r", a=GROUPS), in_=ident[:].rearrange("p (a r) -> p a r", a=GROUPS)
         )
         shifted = const.tile([P, B * W * H, KC], F32)
-        for j in range(4):
-            nc.vector.memset(shifted[:, 8 * j : 8 * j + 8, :], 0.0)
-        outflat = out.rearrange("b h w u c -> (b h w u c)")
+        nc.vector.memset(shifted[:], 0.0)
         stages = []
-        for n in range(4):
-            stage = const.tile([P, H, PITCH], F32, name="stage%d" % n)
+        for n in range(2):
+            stage = const.tile([P, 2 * H, PITCH], F32, name="stage%d" % n)
             nc.vector.memset(stage[:, :, F:PITCH], 0.0)
             stages.append(stage)
 
-        qcodes = const.tile([P, B * W, H * U], U32, align_bytes=64)
-        qscales = const.tile([P, B * W, H * U], U8, align_bytes=64)
+        qcodes = const.tile([P, N_Q, 2 * H * U], U32, align_bytes=64)
+        qscales = const.tile([P, N_Q, 2 * H * U], U8, align_bytes=64)
         scodes = const.tile([P, 4 * F], U32, align_bytes=64)
         sscales = const.tile([P, 4 * F], U8, align_bytes=64)
         pcodes = const.tile([P, H * F], U32, align_bytes=64)
         pscales = const.tile([P, H * F], U8, align_bytes=64)
 
-        counter = [0]
-
-        def transpose_bank(words, first, eye):
-            bank = psum_t.tile([P, 2, 2, P], F32, tag="xt")
-            for x in range(2):
-                for u in range(2):
-                    j = first + 2 * x + u
-                    nc.tensor.transpose(bank[:, x, u, :], words[:, j * P : (j + 1) * P], eye[:])
-            return bank
-
-        def evacuate(dst, bank, vector_every):
-            src = bank[:].rearrange("p x u r -> p x r u")
-            counter[0] += 1
-            if vector_every and counter[0] % vector_every == 0:
+        def copy_out(on_vector, dst, src):
+            if on_vector:
                 nc.vector.tensor_copy(out=dst, in_=src)
             else:
                 nc.scalar.copy(out=dst, in_=src)
 
-        sraw = const.tile([P, CH], BF16)
-        nc.sync.dma_start(out=sraw[:], in_=sin_emb)
-        gs = grp.tile([P, 4, P, 4], BF16, tag="gq", align_bytes=64)
+        def transpose_rows(words, first, eye, dst, on_vector):
+            bank = psum_t.tile([P, 2, 2, P], F32, name="xt", tag="xt")
+            for x in range(2):
+                for u in range(2):
+                    j = first + 2 * x + u
+                    nc.tensor.transpose(bank[:, x, u, :], words[:, j * P : (j + 1) * P], eye[:])
+            copy_out(on_vector, dst, bank[:].rearrange("p x u r -> p x r u"))
+
+        def transpose_keys(t, h, dst, on_vector):
+            bank = psum_t.tile([P, 2, 2, P], F32, name="xt", tag="xt")
+            for e in range(2):
+                for u in range(2):
+                    j = 2 * h + u
+                    nc.tensor.transpose(bank[:, e, u, :], raw[t][:, e, :].bitcast(F32)[:, j * P : (j + 1) * P], ident[:])
+            copy_out(on_vector, dst, bank[:].rearrange("p e u r -> p r e u"))
+
+        def transpose(t):
+            grouped[t] = grp.tile([P, 4, 2 * P, 4], BF16, name="grouped", tag="grouped", align_bytes=64)
+            words = grouped[t][:].bitcast(F32)
+            for n in range(4):
+                if t < N_W + N_Q:
+                    dst = words[:, n, :, :].rearrange("p (x r) u -> p x r u", x=2)
+                    eye = ident if t < N_W else perm
+                    on_vector = n == 3 if t < N_W else n >= 2
+                    transpose_rows(raw[t][:, n // 2, :].bitcast(F32), 4 * (n % 2), eye, dst, on_vector)
+                else:
+                    dst = words[:, n, :, :].rearrange("p (r e) u -> p r e u", e=2)
+                    transpose_keys(t, n, dst, False)
+
+        def quantise(t):
+            if N_W <= t < N_W + N_Q:
+                codes[t], scales[t] = qcodes[:, t - N_W, :], qscales[:, t - N_W, :]
+            else:
+                ctile = cod.tile([P, 8 * P], U32, name="ctile", tag="ctile", align_bytes=64)
+                stile = cod.tile([P, 8 * P], U8, name="stile", tag="stile", align_bytes=64)
+                codes[t], scales[t] = ctile[:], stile[:]
+            for n in range(2):
+                cols = slice(4 * P * n, 4 * P * (n + 1))
+                nc.vector.quantize_mx(
+                    out=codes[t][:, cols].bitcast(FP8X4),
+                    scales=scales[t][:, cols],
+                    in_=grouped[t][:, 2 * n : 2 * n + 2].rearrange("p n c t -> p (n c t)"),
+                )
+
+        def mx(dst, t_l, l0, t_r, r0, n, start, stop):
+            nc.tensor.matmul_mx(
+                out=dst,
+                lhsT=codes[t_l][:, l0 : l0 + P].bitcast(FP8X4),
+                lhsT_scale=scales[t_l][:, l0 : l0 + P],
+                rhs=codes[t_r][:, r0 : r0 + n].bitcast(FP8X4),
+                rhs_scale=scales[t_r][:, r0 : r0 + n],
+                start=start,
+                stop=stop,
+            )
+
+        def multiply(t):
+            if t < N_W:
+                if t % 2 == 0:
+                    banks["p"] = psum_a.tile([P, 4, F], F32, name="acc", tag="acc")
+                for e in range(2):
+                    for c in range(4):
+                        mx(banks["p"][:, 2 * (t % 2) + e, :], t, (4 * e + c) * P, "sin", c * P, F, c == 0, c == 3)
+            elif t < N_W + N_Q:
+                for s in range(2):
+                    banks[s] = psum_a.tile([P, H, F], F32, name="acc", tag="acc")
+                    for h in range(H):
+                        mx(banks[s][:, h, :], t, (H * s + h) * P, "proj", h * P, F, True, True)
+            else:
+                bw = t - N_W - N_Q
+                for i in range(2):
+                    banks[i] = psum_a.tile([P, 2, KC], F32, name="acc", tag="acc")
+                    for x in range(2):
+                        h = 2 * i + x
+                        mx(banks[i][:, x, :], N_W + bw // 2, (H * (bw % 2) + h) * P, t, h * KC, KC, True, True)
+
+        def finish(t):
+            if t < N_W:
+                if t % 2 == 0:
+                    return
+                hcols = slice((t // 2) * P, (t // 2 + 1) * P)
+                pg = grp.tile([P, F, 4], BF16, name="pg", tag="pg", align_bytes=64)
+                nc.vector.tensor_copy(out=pg[:], in_=banks["p"][:].rearrange("p t f -> p f t"))
+                nc.vector.quantize_mx(
+                    out=pcodes[:, hcols].bitcast(FP8X4), scales=pscales[:, hcols], in_=pg[:].rearrange("p f t -> p (f t)")
+                )
+            elif t < N_W + N_Q:
+                j = t - N_W
+                stage = stages[j % 2]
+                for s in range(2):
+                    nc.scalar.copy(out=stage[:, H * s : H * (s + 1), 0:F], in_=banks[s][:])
+                first = SCRATCH + j * PAIR
+                nc.scalar.dma_start(
+                    out=outflat[first : first + PAIR].rearrange("(u y) -> u y", y=PAIR_ROW),
+                    in_=stage[:].rearrange("p k x -> p (k x)"),
+                )
+            else:
+                bw = t - N_W - N_Q
+                total = outp.tile([P, H, KC], F32, name="total", tag="total")
+                for i in range(2):
+                    nc.vector.tensor_tensor(
+                        out=total[:, 2 * i : 2 * i + 2, :],
+                        in0=banks[i][:],
+                        in1=shifted[:, bw * H + 2 * i : bw * H + 2 * i + 2, :],
+                        op=mybir.AluOpType.add,
+                    )
+                for a in range(GROUPS):
+                    nc.sync.dma_start(
+                        out=out[bw // W, :, bw % W, a * QUAD : (a + 1) * QUAD, :].rearrange("h r c -> r h c"),
+                        in_=total[a:P:GROUPS, :, :],
+                    )
+
+        def read_back(t):
+            j = t - N_W
+            for a in range(GROUPS):
+                first = SCRATCH + j * PAIR + a * PAIR_ROW
+                rows = outflat[first : first + QUAD * (GROUPS * PAIR_ROW - 1)].rearrange(
+                    "(r y) -> r y", y=GROUPS * PAIR_ROW - 1
+                )
+                nc.sync.dma_start(
+                    out=shifted[a:P:GROUPS, 2 * H * j : 2 * H * (j + 1), a * QUAD : a * QUAD + WIN],
+                    in_=rows[:, 0:PAIR_ROW].rearrange("r (k x) -> r k x", x=PITCH)[:, :, 0:WIN],
+                )
+
+        gs = const.tile([P, 4, P, 4], BF16, align_bytes=64)
         for i in range(2):
-            bank = transpose_bank(sraw[:].bitcast(F32), 4 * i, ident)
-            evacuate(gs[:].bitcast(F32)[:, 2 * i : 2 * i + 2, :, :], bank, 2)
+            transpose_rows(sraw[:].bitcast(F32), 4 * i, ident, gs[:].bitcast(F32)[:, 2 * i : 2 * i + 2, :, :], i == 1)
         nc.vector.quantize_mx(
             out=scodes[:].bitcast(FP8X4), scales=sscales[:], in_=gs[:].rearrange("p c r t -> p (c r t)")
         )
+        codes["sin"], scales["sin"] = scodes[:], sscales[:]
+        codes["proj"], scales["proj"] = pcodes[:], pscales[:]
 
-        pbank = None
-        for g in range(8):
-            h = g // 2
-            wraw = raw.tile([P, 2, CH], BF16, tag="raw8")
-            nc.sync.dma_start(out=wraw[:], in_=pos_w[256 * g : 256 * (g + 1), :].rearrange("(p e) c -> p e c", e=2))
-            gw = grp.tile([P, 2, 4, P, 4], BF16, tag="gw", align_bytes=64)
-            wcodes = cod.tile([P, 2, 4 * P], U32, align_bytes=64)
-            wscales = cod.tile([P, 2, 4 * P], U8, align_bytes=64)
-            if g % 2 == 0:
-                pbank = psum_a.tile([P, 4, F], F32, tag="acc")
-            for e in range(2):
-                for i in range(2):
-                    bank = transpose_bank(wraw[:, e, :].bitcast(F32), 4 * i, ident)
-                    evacuate(gw[:, e].bitcast(F32)[:, 2 * i : 2 * i + 2, :, :], bank, 4)
-                nc.vector.quantize_mx(
-                    out=wcodes[:, e, :].bitcast(FP8X4),
-                    scales=wscales[:, e, :],
-                    in_=gw[:, e].rearrange("p c r t -> p (c r t)"),
-                )
-            for e in range(2):
-                t = 2 * (g % 2) + e
-                for c in range(4):
-                    cols = slice(c * P, (c + 1) * P)
-                    nc.tensor.matmul_mx(
-                        out=pbank[:, t, :],
-                        lhsT=wcodes[:, e, cols].bitcast(FP8X4),
-                        lhsT_scale=wscales[:, e, cols],
-                        rhs=scodes[:, cols].bitcast(FP8X4),
-                        rhs_scale=sscales[:, cols],
-                        start=(c == 0),
-                        stop=(c == 3),
-                    )
-            if g % 2 == 0:
-                continue
-            hcols = slice(h * P, (h + 1) * P)
-            pg = grp.tile([P, F, 4], BF16, tag="pg", align_bytes=64)
-            nc.vector.tensor_copy(out=pg[:], in_=pbank[:].rearrange("p t f -> p f t"))
-            nc.vector.quantize_mx(
-                out=pcodes[:, hcols].bitcast(FP8X4), scales=pscales[:, hcols], in_=pg[:].rearrange("p f t -> p (f t)")
-            )
-
-        for bw in range(B * W):
-            qraw = qin.tile([P, CH], BF16)
-            nc.sync.dma_start(out=qraw[:], in_=queries[bw // W, bw % W].rearrange("u h d -> u (h d)"))
-            gq = grp.tile([P, H, P, 4], BF16, tag="gq", align_bytes=64)
-            for i in range(2):
-                bank = transpose_bank(qraw[:].bitcast(F32), 4 * i, perm)
-                evacuate(gq[:].bitcast(F32)[:, 2 * i : 2 * i + 2, :, :], bank, 2)
-            nc.vector.quantize_mx(
-                out=qcodes[:, bw, :].bitcast(FP8X4),
-                scales=qscales[:, bw, :],
-                in_=gq[:].rearrange("p h r t -> p (h r t)"),
-            )
-
-            bdbank = psum_a.tile([P, H, F], F32, tag="acc")
-            for h in range(H):
-                hcols = slice(h * P, (h + 1) * P)
-                nc.tensor.matmul_mx(
-                    out=bdbank[:, h, :],
-                    lhsT=qcodes[:, bw, hcols].bitcast(FP8X4),
-                    lhsT_scale=qscales[:, bw, hcols],
-                    rhs=pcodes[:, hcols].bitcast(FP8X4),
-                    rhs_scale=pscales[:, hcols],
-                    start=True,
-                    stop=True,
-                )
-            stage = stages[bw % 4]
-            nc.scalar.copy(out=stage[:, :, 0:F], in_=bdbank[:])
-            first = SCRATCH + bw * H * BLOCK
-            nc.scalar.dma_start(
-                out=outflat[first : first + H * BLOCK].rearrange("(h u x) -> u h x", h=H, x=PITCH), in_=stage[:]
-            )
-            if bw % 2 == 0:
-                continue
-            first = SCRATCH + (bw - 1) * H * BLOCK
-            rows = (
-                outflat[first : first + 2 * H * BLOCK]
-                .rearrange("(k y) -> k y", k=2 * H)[:, 0 : QUAD * (GROUPS * PITCH - 1)]
-                .rearrange("k (r x) -> r k x", x=GROUPS * PITCH - 1)
-            )
-            for a in range(GROUPS):
-                nc.sync.dma_start(
-                    out=shifted[a:P:GROUPS, (bw - 1) * H : (bw + 1) * H, a * QUAD : a * QUAD + WIN],
-                    in_=rows[:, :, a * PITCH : a * PITCH + WIN],
-                )
-
-        for bw in range(B * W):
-            b, w = bw // W, bw % W
-            kraw = raw.tile([P, 2, CH], BF16, tag="raw8")
-            nc.sync.dma_start(out=kraw[:], in_=keys[b, w].rearrange("(e p) h d -> p e (h d)", e=2))
-            total = outp.tile([P, H, KC], F32)
-            for i in range(2):
-                gk = grp.tile([P, 2, KC, 4], BF16, tag="gk", bufs=3, align_bytes=64)
-                for e in range(2):
-                    bank = transpose_bank(kraw[:, e, :].bitcast(F32), 4 * i, ident)
-                    evacuate(gk[:].bitcast(F32)[:, :, e * P : (e + 1) * P, :], bank, 0)
-                kcodes = kcd.tile([P, 2 * KC], U32, align_bytes=64)
-                kscales = kcd.tile([P, 2 * KC], U8, align_bytes=64)
-                nc.vector.quantize_mx(
-                    out=kcodes[:].bitcast(FP8X4), scales=kscales[:], in_=gk[:].rearrange("p x c t -> p (x c t)")
-                )
-                acbank = psum_a.tile([P, 2, KC], F32, tag="acc")
-                for x in range(2):
-                    hcols = slice((2 * i + x) * P, (2 * i + x + 1) * P)
-                    kcols = slice(x * KC, (x + 1) * KC)
-                    nc.tensor.matmul_mx(
-                        out=acbank[:, x, :],
-                        lhsT=qcodes[:, bw, hcols].bitcast(FP8X4),
-                        lhsT_scale=qscales[:, bw, hcols],
-                        rhs=kcodes[:, kcols].bitcast(FP8X4),
-                        rhs_scale=kscales[:, kcols],
-                        start=True,
-                        stop=True,
-                    )
-                nc.vector.tensor_tensor(
-                    out=total[:, 2 * i : 2 * i + 2, :],
-                    in0=acbank[:],
-                    in1=shifted[:, bw * H + 2 * i : bw * H + 2 * i + 2, :],
-                    op=mybir.AluOpType.add,
-                )
-            for a in range(GROUPS):
-                nc.sync.dma_start(
-                    out=out[b, :, w, a * QUAD : (a + 1) * QUAD, :].rearrange("h r c -> r h c"), in_=total[a:P:GROUPS, :, :]
-                )
+        for t in range(N_TILES + 3):
+            if 1 <= t <= N_TILES:
+                quantise(t - 1)
+            if t < N_TILES:
+                transpose(t)
+            if t + DEPTH < N_TILES:
+                load(t + DEPTH)
+            if 1 <= t <= N_TILES:
+                multiply(t - 1)
+                finish(t - 1)
+            if N_W <= t - 3 < N_W + N_Q:
+                read_back(t - 3)

@@ -22,7 +22,7 @@ SCRATCH = B * H * W * U * KC - 4 * PAIR - 4096
 
 N_W, N_Q, N_K = 8, 4, 8
 N_TILES = N_W + N_Q + N_K
-DEPTH = 8
+DEPTH = 4
 
 FLOPS = 2 * F * CH * CH + B * W * H * 2 * U * D * (KC + F)
 
@@ -66,7 +66,6 @@ def tile_gemma3naudiorelativepositionembedding_pa_kernel(tc, queries, keys, sin_
             out=perm[:].rearrange("p (r a) -> p a r", a=GROUPS), in_=ident[:].rearrange("p (a r) -> p a r", a=GROUPS)
         )
         shifted = const.tile([P, B * W * H, KC], F32)
-        nc.vector.memset(shifted[:], 0.0)
         stages = []
         for n in range(2):
             stage = const.tile([P, 2 * H, PITCH], F32, name="stage%d" % n)
@@ -109,7 +108,7 @@ def tile_gemma3naudiorelativepositionembedding_pa_kernel(tc, queries, keys, sin_
                 if t < N_W + N_Q:
                     dst = words[:, n, :, :].rearrange("p (x r) u -> p x r u", x=2)
                     eye = ident if t < N_W else perm
-                    on_vector = n == 3 if t < N_W else n >= 2
+                    on_vector = t >= N_W and n >= 2
                     transpose_rows(raw[t][:, n // 2, :].bitcast(F32), 4 * (n % 2), eye, dst, on_vector)
                 else:
                     dst = words[:, n, :, :].rearrange("p (r e) u -> p r e u", e=2)
@@ -144,22 +143,22 @@ def tile_gemma3naudiorelativepositionembedding_pa_kernel(tc, queries, keys, sin_
         def multiply(t):
             if t < N_W:
                 if t % 2 == 0:
-                    banks["p"] = psum_a.tile([P, 4, F], F32, name="acc", tag="acc")
+                    banks[t + 1] = psum_a.tile([P, 4, F], F32, name="acc", tag="acc")
                 for e in range(2):
                     for c in range(4):
-                        mx(banks["p"][:, 2 * (t % 2) + e, :], t, (4 * e + c) * P, "sin", c * P, F, c == 0, c == 3)
+                        mx(banks[t | 1][:, 2 * (t % 2) + e, :], t, (4 * e + c) * P, "sin", c * P, F, c == 0, c == 3)
             elif t < N_W + N_Q:
                 for s in range(2):
-                    banks[s] = psum_a.tile([P, H, F], F32, name="acc", tag="acc")
+                    banks[(t, s)] = psum_a.tile([P, H, F], F32, name="acc", tag="acc")
                     for h in range(H):
-                        mx(banks[s][:, h, :], t, (H * s + h) * P, "proj", h * P, F, True, True)
+                        mx(banks[(t, s)][:, h, :], t, (H * s + h) * P, "proj", h * P, F, True, True)
             else:
                 bw = t - N_W - N_Q
                 for i in range(2):
-                    banks[i] = psum_a.tile([P, 2, KC], F32, name="acc", tag="acc")
+                    banks[(t, i)] = psum_a.tile([P, 2, KC], F32, name="acc", tag="acc")
                     for x in range(2):
                         h = 2 * i + x
-                        mx(banks[i][:, x, :], N_W + bw // 2, (H * (bw % 2) + h) * P, t, h * KC, KC, True, True)
+                        mx(banks[(t, i)][:, x, :], N_W + bw // 2, (H * (bw % 2) + h) * P, t, h * KC, KC, True, True)
 
         def finish(t):
             if t < N_W:
@@ -167,7 +166,7 @@ def tile_gemma3naudiorelativepositionembedding_pa_kernel(tc, queries, keys, sin_
                     return
                 hcols = slice((t // 2) * P, (t // 2 + 1) * P)
                 pg = grp.tile([P, F, 4], BF16, name="pg", tag="pg", align_bytes=64)
-                nc.vector.tensor_copy(out=pg[:], in_=banks["p"][:].rearrange("p t f -> p f t"))
+                nc.vector.tensor_copy(out=pg[:], in_=banks[t][:].rearrange("p t f -> p f t"))
                 nc.vector.quantize_mx(
                     out=pcodes[:, hcols].bitcast(FP8X4), scales=pscales[:, hcols], in_=pg[:].rearrange("p f t -> p (f t)")
                 )
@@ -175,7 +174,7 @@ def tile_gemma3naudiorelativepositionembedding_pa_kernel(tc, queries, keys, sin_
                 j = t - N_W
                 stage = stages[j % 2]
                 for s in range(2):
-                    nc.scalar.copy(out=stage[:, H * s : H * (s + 1), 0:F], in_=banks[s][:])
+                    nc.scalar.copy(out=stage[:, H * s : H * (s + 1), 0:F], in_=banks[(t, s)][:])
                 first = SCRATCH + j * PAIR
                 nc.scalar.dma_start(
                     out=outflat[first : first + PAIR].rearrange("(u y) -> u y", y=PAIR_ROW),
@@ -187,7 +186,7 @@ def tile_gemma3naudiorelativepositionembedding_pa_kernel(tc, queries, keys, sin_
                 for i in range(2):
                     nc.vector.tensor_tensor(
                         out=total[:, 2 * i : 2 * i + 2, :],
-                        in0=banks[i][:],
+                        in0=banks[(t, i)][:],
                         in1=shifted[:, bw * H + 2 * i : bw * H + 2 * i + 2, :],
                         op=mybir.AluOpType.add,
                     )
@@ -218,15 +217,18 @@ def tile_gemma3naudiorelativepositionembedding_pa_kernel(tc, queries, keys, sin_
         codes["sin"], scales["sin"] = scodes[:], sscales[:]
         codes["proj"], scales["proj"] = pcodes[:], pscales[:]
 
-        for t in range(N_TILES + 3):
+        for t in range(N_TILES + 2):
             if 1 <= t <= N_TILES:
                 quantise(t - 1)
+            if t < N_W:
+                nc.vector.memset(shifted[:, H * t : H * (t + 1), :], 0.0)
+            if t >= 2:
+                finish(t - 2)
+            if N_W <= t - 4 < N_W + N_Q:
+                read_back(t - 4)
             if t < N_TILES:
                 transpose(t)
             if t + DEPTH < N_TILES:
                 load(t + DEPTH)
             if 1 <= t <= N_TILES:
                 multiply(t - 1)
-                finish(t - 1)
-            if N_W <= t - 3 < N_W + N_Q:
-                read_back(t - 3)

@@ -22,7 +22,7 @@ SCRATCH = B * H * W * U * KC - 4 * PAIR - 4096
 
 N_W, N_Q, N_K = 8, 4, 8
 N_TILES = N_W + N_Q + N_K
-DEPTH = 4
+DEPTH = 6
 
 FLOPS = 2 * F * CH * CH + B * W * H * 2 * U * D * (KC + F)
 

@@ -65,11 +65,11 @@ def tile_gemma3naudiorelativepositionembedding_pa_kernel(tc, queries, keys, sin_
         nc.vector.tensor_copy(
             out=perm[:].rearrange("p (r a) -> p a r", a=GROUPS), in_=ident[:].rearrange("p (a r) -> p a r", a=GROUPS)
         )
-        shifted = const.tile([P, B * W * H, KC], F32)
+        shifted = const.tile([P, N_Q, KC, 2 * H], F32)
         stages = []
         for n in range(2):
-            stage = const.tile([P, 2 * H, PITCH], F32, name="stage%d" % n)
-            nc.vector.memset(stage[:, :, F:PITCH], 0.0)
+            stage = const.tile([P, PITCH, 2 * H], F32, name="stage%d" % n)
+            nc.vector.memset(stage[:, F:PITCH, :], 0.0)
             stages.append(stage)
 
         qcodes = const.tile([P, N_Q, 2 * H * U], U32, align_bytes=64)
@@ -174,20 +174,21 @@ def tile_gemma3naudiorelativepositionembedding_pa_kernel(tc, queries, keys, sin_
                 j = t - N_W
                 stage = stages[j % 2]
                 for s in range(2):
-                    nc.scalar.copy(out=stage[:, H * s : H * (s + 1), 0:F], in_=banks[(t, s)][:])
+                    nc.scalar.copy(out=stage[:, 0:F, H * s : H * (s + 1)], in_=banks[(t, s)][:].rearrange("p h f -> p f h"))
                 first = SCRATCH + j * PAIR
                 nc.scalar.dma_start(
                     out=outflat[first : first + PAIR].rearrange("(u y) -> u y", y=PAIR_ROW),
-                    in_=stage[:].rearrange("p k x -> p (k x)"),
+                    in_=stage[:].rearrange("p x k -> p (x k)"),
                 )
             else:
                 bw = t - N_W - N_Q
                 total = outp.tile([P, H, KC], F32, name="total", tag="total")
                 for i in range(2):
+                    k = H * (bw % 2) + 2 * i
                     nc.vector.tensor_tensor(
-                        out=total[:, 2 * i : 2 * i + 2, :],
-                        in0=banks[(t, i)][:],
-                        in1=shifted[:, bw * H + 2 * i : bw * H + 2 * i + 2, :],
+                        out=total[:, 2 * i : 2 * i + 2, :].rearrange("p x c -> p c x"),
+                        in0=banks[(t, i)][:].rearrange("p x c -> p c x"),
+                        in1=shifted[:, bw // 2, :, k : k + 2],
                         op=mybir.AluOpType.add,
                     )
                 for a in range(GROUPS):
@@ -200,12 +201,11 @@ def tile_gemma3naudiorelativepositionembedding_pa_kernel(tc, queries, keys, sin_
             j = t - N_W
             for a in range(GROUPS):
                 first = SCRATCH + j * PAIR + a * PAIR_ROW
-                rows = outflat[first : first + QUAD * (GROUPS * PAIR_ROW - 1)].rearrange(
-                    "(r y) -> r y", y=GROUPS * PAIR_ROW - 1
-                )
+                step = GROUPS * PAIR_ROW - 2 * H
+                rows = outflat[first : first + QUAD * step].rearrange("(r y) -> r y", y=step)
                 nc.sync.dma_start(
-                    out=shifted[a:P:GROUPS, 2 * H * j : 2 * H * (j + 1), a * QUAD : a * QUAD + WIN],
-                    in_=rows[:, 0:PAIR_ROW].rearrange("r (k x) -> r k x", x=PITCH)[:, :, 0:WIN],
+                    out=shifted[a:P:GROUPS, j, a * QUAD : a * QUAD + WIN, :].rearrange("p x k -> p (x k)"),
+                    in_=rows[:, 0 : WIN * 2 * H],
                 )
 
         gs = const.tile([P, 4, P, 4], BF16, align_bytes=64)
@@ -221,7 +221,7 @@ def tile_gemma3naudiorelativepositionembedding_pa_kernel(tc, queries, keys, sin_
             if 1 <= t <= N_TILES:
                 quantise(t - 1)
             if t < N_W:
-                nc.vector.memset(shifted[:, H * t : H * (t + 1), :], 0.0)
+                nc.vector.memset(shifted[:, t // 2, P * (t % 2) : P * (t % 2 + 1), :], 0.0)
             if t >= 2:
                 finish(t - 2)
             if N_W <= t - 4 < N_W + N_Q:

@@ -203,10 +203,11 @@ def tile_gemma3naudiorelativepositionembedding_pa_kernel(tc, queries, keys, sin_
                 first = SCRATCH + j * PAIR + a * PAIR_ROW
                 step = GROUPS * PAIR_ROW - 2 * H
                 rows = outflat[first : first + QUAD * step].rearrange("(r y) -> r y", y=step)
-                nc.sync.dma_start(
-                    out=shifted[a:P:GROUPS, j, a * QUAD : a * QUAD + WIN, :].rearrange("p x k -> p (x k)"),
-                    in_=rows[:, 0 : WIN * 2 * H],
-                )
+                for x0, x1 in ((0, 80), (80, WIN)):
+                    nc.sync.dma_start(
+                        out=shifted[a:P:GROUPS, j, a * QUAD + x0 : a * QUAD + x1, :].rearrange("p x k -> p (x k)"),
+                        in_=rows[:, x0 * 2 * H : x1 * 2 * H],
+                    )
 
         gs = const.tile([P, 4, P, 4], BF16, align_bytes=64)
         for i in range(2):

from contextlib import ExitStack

import concourse.mybir as mybir
from concourse.masks import make_identity

F32 = mybir.dt.float32
BF16 = mybir.dt.bfloat16
U32 = mybir.dt.uint32
U8 = mybir.dt.uint8
FP8X4 = mybir.dt.float8_e4m3fn_x4

P = 128
B, W, U, H, D, KC, F = 2, 4, 128, 4, 512, 256, 128
CH = H * D
PITCH = 160
WIN = PITCH - 1
QUAD = 32
GROUPS = U // QUAD
PAIR_ROW = 2 * H * PITCH
PAIR = U * PAIR_ROW
SCRATCH = B * H * W * U * KC - 4 * PAIR - 4096

N_W, N_Q, N_K = 8, 4, 8
N_TILES = N_W + N_Q + N_K
DEPTH = 6

FLOPS = 2 * F * CH * CH + B * W * H * 2 * U * D * (KC + F)


def tile_gemma3naudiorelativepositionembedding_pa_kernel(tc, queries, keys, sin_emb, pos_w, out):
    nc = tc.nc
    with ExitStack() as ctx:
        const = ctx.enter_context(tc.tile_pool(name="const", bufs=1))
        rawp = ctx.enter_context(tc.tile_pool(name="rawp", bufs=DEPTH))
        grp = ctx.enter_context(tc.tile_pool(name="grp", bufs=3))
        cod = ctx.enter_context(tc.tile_pool(name="cod", bufs=3))
        outp = ctx.enter_context(tc.tile_pool(name="outp", bufs=3))
        psum_t = ctx.enter_context(tc.psum_pool(name="psumt", bufs=4))
        psum_a = ctx.enter_context(tc.psum_pool(name="psuma", bufs=4))
        ctx.enter_context(tc.manual_schedule())

        outflat = out.rearrange("b h w u c -> (b h w u c)")
        raw, grouped, codes, scales, banks = {}, {}, {}, {}, {}

        def load(t):
            raw[t] = rawp.tile([P, 2, CH], BF16, name="raw", tag="raw")
            if t < N_W:
                src = pos_w[256 * t : 256 * (t + 1), :].rearrange("(p e) c -> p e c", e=2)
            elif t < N_W + N_Q:
                j = t - N_W
                src = queries[j // 2, 2 * (j % 2) : 2 * (j % 2) + 2].rearrange("s u h d -> u s (h d)")
            else:
                bw = t - N_W - N_Q
                src = keys[bw // W, bw % W].rearrange("(p e) h d -> p e (h d)", e=2)
            nc.sync.dma_start(out=raw[t][:], in_=src)

        sraw = const.tile([P, CH], BF16)
        nc.sync.dma_start(out=sraw[:], in_=sin_emb)
        for t in range(DEPTH):
            load(t)

        ident = const.tile([P, P], F32)
        make_identity(nc, ident[:])
        perm = const.tile([P, P], F32)
        nc.vector.tensor_copy(
            out=perm[:].rearrange("p (r a) -> p a r", a=GROUPS), in_=ident[:].rearrange("p (a r) -> p a r", a=GROUPS)
        )
        shifted = const.tile([P, N_Q, KC, 2 * H], F32)
        stages = []
        for n in range(2):
            stage = const.tile([P, PITCH, 2 * H], F32, name="stage%d" % n)
            nc.vector.memset(stage[:, F:PITCH, :], 0.0)
            stages.append(stage)

        qcodes = const.tile([P, N_Q, 2 * H * U], U32, align_bytes=64)
        qscales = const.tile([P, N_Q, 2 * H * U], U8, align_bytes=64)
        scodes = const.tile([P, 4 * F], U32, align_bytes=64)
        sscales = const.tile([P, 4 * F], U8, align_bytes=64)
        pcodes = const.tile([P, H * F], U32, align_bytes=64)
        pscales = const.tile([P, H * F], U8, align_bytes=64)

        def copy_out(on_vector, dst, src):
            if on_vector:
                nc.vector.tensor_copy(out=dst, in_=src)
            else:
                nc.scalar.copy(out=dst, in_=src)

        def transpose_rows(words, first, eye, dst, on_vector):
            bank = psum_t.tile([P, 2, 2, P], F32, name="xt", tag="xt")
            for x in range(2):
                for u in range(2):
                    j = first + 2 * x + u
                    nc.tensor.transpose(bank[:, x, u, :], words[:, j * P : (j + 1) * P], eye[:])
            copy_out(on_vector, dst, bank[:].rearrange("p x u r -> p x r u"))

        def transpose_keys(t, h, dst, on_vector):
            bank = psum_t.tile([P, 2, 2, P], F32, name="xt", tag="xt")
            for e in range(2):
                for u in range(2):
                    j = 2 * h + u
                    nc.tensor.transpose(bank[:, e, u, :], raw[t][:, e, :].bitcast(F32)[:, j * P : (j + 1) * P], ident[:])
            copy_out(on_vector, dst, bank[:].rearrange("p e u r -> p r e u"))

        def transpose(t):
            grouped[t] = grp.tile([P, 4, 2 * P, 4], BF16, name="grouped", tag="grouped", align_bytes=64)
            words = grouped[t][:].bitcast(F32)
            for n in range(4):
                if t < N_W + N_Q:
                    dst = words[:, n, :, :].rearrange("p (x r) u -> p x r u", x=2)
                    eye = ident if t < N_W else perm
                    on_vector = t >= N_W and n >= 2
                    transpose_rows(raw[t][:, n // 2, :].bitcast(F32), 4 * (n % 2), eye, dst, on_vector)
                else:
                    dst = words[:, n, :, :].rearrange("p (r e) u -> p r e u", e=2)
                    transpose_keys(t, n, dst, False)

        def quantise(t):
            if N_W <= t < N_W + N_Q:
                codes[t], scales[t] = qcodes[:, t - N_W, :], qscales[:, t - N_W, :]
            else:
                ctile = cod.tile([P, 8 * P], U32, name="ctile", tag="ctile", align_bytes=64)
                stile = cod.tile([P, 8 * P], U8, name="stile", tag="stile", align_bytes=64)
                codes[t], scales[t] = ctile[:], stile[:]
            for n in range(2):
                cols = slice(4 * P * n, 4 * P * (n + 1))
                nc.vector.quantize_mx(
                    out=codes[t][:, cols].bitcast(FP8X4),
                    scales=scales[t][:, cols],
                    in_=grouped[t][:, 2 * n : 2 * n + 2].rearrange("p n c t -> p (n c t)"),
                )

        def mx(dst, t_l, l0, t_r, r0, n, start, stop):
            nc.tensor.matmul_mx(
                out=dst,
                lhsT=codes[t_l][:, l0 : l0 + P].bitcast(FP8X4),
                lhsT_scale=scales[t_l][:, l0 : l0 + P],
                rhs=codes[t_r][:, r0 : r0 + n].bitcast(FP8X4),
                rhs_scale=scales[t_r][:, r0 : r0 + n],
                start=start,
                stop=stop,
            )

        def multiply(t):
            if t < N_W:
                if t % 2 == 0:
                    banks[t + 1] = psum_a.tile([P, 4, F], F32, name="acc", tag="acc")
                for e in range(2):
                    for c in range(4):
                        mx(banks[t | 1][:, 2 * (t % 2) + e, :], t, (4 * e + c) * P, "sin", c * P, F, c == 0, c == 3)
            elif t < N_W + N_Q:
                for s in range(2):
                    banks[(t, s)] = psum_a.tile([P, H, F], F32, name="acc", tag="acc")
                    for h in range(H):
                        mx(banks[(t, s)][:, h, :], t, (H * s + h) * P, "proj", h * P, F, True, True)
            else:
                bw = t - N_W - N_Q
                for i in range(2):
                    banks[(t, i)] = psum_a.tile([P, 2, KC], F32, name="acc", tag="acc")
                    for x in range(2):
                        h = 2 * i + x
                        mx(banks[(t, i)][:, x, :], N_W + bw // 2, (H * (bw % 2) + h) * P, t, h * KC, KC, True, True)

        def finish(t):
            if t < N_W:
                if t % 2 == 0:
                    return
                hcols = slice((t // 2) * P, (t // 2 + 1) * P)
                pg = grp.tile([P, F, 4], BF16, name="pg", tag="pg", align_bytes=64)
                nc.vector.tensor_copy(out=pg[:], in_=banks[t][:].rearrange("p t f -> p f t"))
                nc.vector.quantize_mx(
                    out=pcodes[:, hcols].bitcast(FP8X4), scales=pscales[:, hcols], in_=pg[:].rearrange("p f t -> p (f t)")
                )
            elif t < N_W + N_Q:
                j = t - N_W
                stage = stages[j % 2]
                for s in range(2):
                    nc.scalar.copy(out=stage[:, 0:F, H * s : H * (s + 1)], in_=banks[(t, s)][:].rearrange("p h f -> p f h"))
                first = SCRATCH + j * PAIR
                nc.scalar.dma_start(
                    out=outflat[first : first + PAIR].rearrange("(u y) -> u y", y=PAIR_ROW),
                    in_=stage[:].rearrange("p x k -> p (x k)"),
                )
            else:
                bw = t - N_W - N_Q
                total = outp.tile([P, H, KC], F32, name="total", tag="total")
                for i in range(2):
                    k = H * (bw % 2) + 2 * i
                    nc.vector.tensor_tensor(
                        out=total[:, 2 * i : 2 * i + 2, :].rearrange("p x c -> p c x"),
                        in0=banks[(t, i)][:].rearrange("p x c -> p c x"),
                        in1=shifted[:, bw // 2, :, k : k + 2],
                        op=mybir.AluOpType.add,
                    )
                for a in range(GROUPS):
                    nc.sync.dma_start(
                        out=out[bw // W, :, bw % W, a * QUAD : (a + 1) * QUAD, :].rearrange("h r c -> r h c"),
                        in_=total[a:P:GROUPS, :, :],
                    )

        def read_back(t):
            j = t - N_W
            for a in range(GROUPS):
                first = SCRATCH + j * PAIR + a * PAIR_ROW
                step = GROUPS * PAIR_ROW - 2 * H
                rows = outflat[first : first + QUAD * step].rearrange("(r y) -> r y", y=step)
                for x0, x1 in ((0, 80), (80, WIN)):
                    nc.sync.dma_start(
                        out=shifted[a:P:GROUPS, j, a * QUAD + x0 : a * QUAD + x1, :].rearrange("p x k -> p (x k)"),
                        in_=rows[:, x0 * 2 * H : x1 * 2 * H],
                    )

        gs = const.tile([P, 4, P, 4], BF16, align_bytes=64)
        for i in range(2):
            transpose_rows(sraw[:].bitcast(F32), 4 * i, ident, gs[:].bitcast(F32)[:, 2 * i : 2 * i + 2, :, :], i == 1)
        nc.vector.quantize_mx(
            out=scodes[:].bitcast(FP8X4), scales=sscales[:], in_=gs[:].rearrange("p c r t -> p (c r t)")
        )
        codes["sin"], scales["sin"] = scodes[:], sscales[:]
        codes["proj"], scales["proj"] = pcodes[:], pscales[:]

        for t in range(N_TILES + 2):
            if 1 <= t <= N_TILES:
                quantise(t - 1)
            if t < N_W:
                nc.vector.memset(shifted[:, t // 2, P * (t % 2) : P * (t % 2 + 1), :], 0.0)
            if t >= 2:
                finish(t - 2)
            if N_W <= t - 4 < N_W + N_Q:
                read_back(t - 4)
            if t < N_TILES:
                transpose(t)
            if t + DEPTH < N_TILES:
                load(t + DEPTH)
            if 1 <= t <= N_TILES:
                multiply(t - 1)
